import numpy as np
import ml_dtypes


def mxq(x, axis, fmt="e4m3"):
    dtype, down = {"e4m3": (ml_dtypes.float8_e4m3fn, 7), "e5m2": (ml_dtypes.float8_e5m2, 14)}[fmt]
    v = np.moveaxis(np.asarray(x, np.float32).astype(ml_dtypes.bfloat16).astype(np.float64), axis, -1)
    blocks = v.reshape(v.shape[:-1] + (-1, 32))
    amax = np.abs(blocks).max(-1, keepdims=True)
    byte = np.maximum(np.where(amax > 0, np.frexp(amax)[1] - 1 + 127, 0) - down, 1)
    scale = np.exp2(byte - 127.0)
    codes = (blocks / scale).astype(np.float32).astype(dtype).astype(np.float64)
    return np.moveaxis((codes * scale).reshape(v.shape), -1, axis)


WIDE = False


def mx_kscale(k):
    if not WIDE:
        return np.ones(k)
    levels = np.array([20, -20, 10, -10, 0])
    a = np.random.permutation(np.resize(levels, k // 512 * 4)).reshape(k // 512, 4)
    idx = np.arange(k)
    return np.exp2(a[idx // 512, idx % 128 // 32])


BF16 = ml_dtypes.bfloat16


def bf(x):
    return np.asarray(x, np.float32).astype(BF16)


def f64(x):
    return np.asarray(x).astype(np.float64)


B, STACK, TUBE, CH, IMG, PATCH, EMBED = 16, 16, 2, 1, 96, 16, 1024
GH = IMG // PATCH
GW = IMG // PATCH
GD = STACK // TUBE
N = GD * GH * GW
T = B * N
K = TUBE * CH * PATCH * PATCH


def _sincos_1d(dim, pos):
    omega = 1.0 / (10000.0 ** (np.arange(dim // 2, dtype=np.float64) / (dim / 2.0)))
    out = pos[:, None].astype(np.float64) * omega[None, :]
    return np.concatenate([np.sin(out), np.cos(out)], axis=1)


def get_3d_sincos_pos_embed(grid_h, grid_w, grid_depth, embed_dim):
    dim_t = embed_dim // 4
    dim_s = embed_dim - dim_t
    emb_t = _sincos_1d(dim_t, np.arange(grid_depth))
    emb_h = _sincos_1d(dim_s // 2, np.arange(grid_h))
    emb_w = _sincos_1d(dim_s - dim_s // 2, np.arange(grid_w))
    emb_hw = np.concatenate([np.repeat(emb_h, grid_w, axis=0), np.tile(emb_w, (grid_h, 1))], axis=1)
    ns = grid_h * grid_w
    return np.concatenate([np.repeat(emb_t, ns, axis=0), np.tile(emb_hw, (grid_depth, 1))], axis=1)


def _tubelets(video):
    B_, T_, C, H, W_ = video.shape
    p = PATCH
    gh, gw = H // p, W_ // p
    ns = gh * gw
    x = video.reshape(B_ * T_, C, gh, p, gw, p)
    x = x.transpose(0, 2, 4, 1, 3, 5)
    x = x.reshape(B_, GD, TUBE, ns, C * p * p)
    x = x.transpose(0, 1, 3, 2, 4)
    return x.reshape(B_, GD * ns, TUBE * C * p * p)


def setup_inputs():
    s = mx_kscale(T)
    sv = s.reshape(B, GD, 1, 1, GH, 1, GW, 1)
    video = np.random.standard_normal((B, GD, TUBE, CH, GH, PATCH, GW, PATCH)) * sv
    W = np.random.standard_normal((EMBED, K)) / np.sqrt(K)
    b = np.random.standard_normal(EMBED) * 0.3
    pos = get_3d_sincos_pos_embed(GH, GW, GD, EMBED)[None]
    g = np.random.standard_normal((B, N, EMBED)) * np.exp2(np.random.randint(-12, 1, (B, N, 1))) * 0.25 / s.reshape(B, N, 1)
    return {"video": bf(video.reshape(B, STACK, CH, IMG, IMG)),
            "W": bf(W),
            "b": bf(b),
            "pos_embed": bf(pos),
            "grad_out": bf(g)}


def reference(video, W, b, pos_embed, grad_out):
    tub = _tubelets(f64(video)).reshape(T, K)
    g = f64(grad_out).reshape(T, EMBED)
    return mxq(g, 0, "e5m2").T @ mxq(tub, 0, "e4m3")

@@ -1,0 +1,163 @@
+from contextlib import ExitStack
+
+import concourse.mybir as mybir
+from concourse.masks import make_identity
+
+BF16 = mybir.dt.bfloat16
+F32 = mybir.dt.float32
+U32 = mybir.dt.uint32
+U8 = mybir.dt.uint8
+E4M3_X4 = mybir.dt.float8_e4m3fn_x4
+E5M2_X4 = mybir.dt.float8_e5m2_x4
+
+P = 128
+PACK = 4
+WINDOW = P * PACK
+
+BATCH = 16
+TUBES = 128
+FRAMES_PER_TUBE = 2
+GRID = 6
+PATCH = 16
+IMAGE_ROW = GRID * PATCH
+TOKENS_PER_TUBE = GRID * GRID
+TOKENS = TUBES * TOKENS_PER_TUBE
+WINDOWS = TOKENS // WINDOW
+EMBED = 1024
+FEATURES = FRAMES_PER_TUBE * PATCH * PATCH
+EMBED_TILES = EMBED // P
+
+WINDOWS_PER_GROUP = P // (PATCH * FRAMES_PER_TUBE)
+GROUPS = -(-WINDOWS // WINDOWS_PER_GROUP)
+PIXEL_PAIRS = PATCH // 2
+LEAD_ROOM = TOKENS_PER_TUBE - PACK
+ROW_SLOTS = 16 * TOKENS_PER_TUBE
+
+FLOPS = 2 * TOKENS * EMBED * FEATURES
+BYTES = 2 * TOKENS * FEATURES + 2 * TOKENS * EMBED + 4 * EMBED * FEATURES
+
+
+def load_window_rows(nc, video_rows, rows, c):
+    x = c % WINDOWS_PER_GROUP
+    first_tube = (c * WINDOW) // TOKENS_PER_TUBE
+    last_tube = (c * WINDOW + WINDOW - 1) // TOKENS_PER_TUBE
+    tubes = last_tube - first_tube + 1
+    lead = c * WINDOW - first_tube * TOKENS_PER_TUBE
+    start = (LEAD_ROOM - lead) * PATCH
+    for i in range(GRID):
+        for ts in range(FRAMES_PER_TUBE):
+            base = x * PATCH * FRAMES_PER_TUBE
+            mine = rows[base + ts : base + PATCH * FRAMES_PER_TUBE : FRAMES_PER_TUBE, :]
+            by_tube = mine[:, start : start + tubes * TOKENS_PER_TUBE * PATCH].rearrange(
+                "y (t r) -> y t r", t=tubes
+            )
+            nc.sync.dma_start(
+                out=by_tube[:, :, i * IMAGE_ROW : (i + 1) * IMAGE_ROW],
+                in_=video_rows[ts, i, :, first_tube : last_tube + 1, :],
+            )
+
+
+def tile_tubeletembedding_kernel(tc, video, W, b, pos_embed, grad_out, out):
+    nc = tc.nc
+    video_rows = video.rearrange("b f c h w -> (b f c h) w").rearrange(
+        "(t s i y) w -> s i y t w", s=FRAMES_PER_TUBE, i=GRID, y=PATCH
+    )
+    grad_rows = grad_out.rearrange("b n e -> (b n) e")
+
+    with ExitStack() as stack:
+        keep = stack.enter_context(tc.tile_pool(name="keep", bufs=1))
+        stage = stack.enter_context(tc.tile_pool(name="stage", bufs=2))
+        grad_in = stack.enter_context(tc.tile_pool(name="grad_in", bufs=4))
+        grad_stage = stack.enter_context(tc.tile_pool(name="grad_stage", bufs=3))
+        results = stack.enter_context(tc.tile_pool(name="results", bufs=4))
+        psum = stack.enter_context(tc.psum_pool(name="psum", bufs=8))
+
+        identity = keep.tile([P, P], F32)
+        make_identity(nc, identity[:])
+
+        tub_codes = keep.tile([P, WINDOWS, FEATURES], U32, align_bytes=64)
+        tub_scales = keep.tile([P, WINDOWS, FEATURES], U8, align_bytes=64)
+        grad_codes = keep.tile([P, WINDOWS, EMBED], U32, align_bytes=64)
+        grad_scales = keep.tile([P, WINDOWS, EMBED], U8, align_bytes=64)
+
+        rows_a = keep.tile([P, ROW_SLOTS * PATCH], BF16)
+        rows_b = keep.tile([P, ROW_SLOTS * PATCH], BF16)
+        rows_of_group = [rows_a, rows_b, rows_a]
+
+        for group in range(GROUPS):
+            rows = rows_of_group[group]
+            first_window = group * WINDOWS_PER_GROUP
+            windows = min(WINDOWS_PER_GROUP, WINDOWS - first_window)
+            for x in range(windows):
+                load_window_rows(nc, video_rows, rows, first_window + x)
+
+            words = (
+                rows[:]
+                .bitcast(F32)[:, LEAD_ROOM * PIXEL_PAIRS : (LEAD_ROOM + WINDOW) * PIXEL_PAIRS]
+                .rearrange("p (m j w) -> p j w m", j=PACK, w=PIXEL_PAIRS)
+            )
+            grouped = stage.tile([P, WINDOWS_PER_GROUP, FEATURES * PACK], BF16, align_bytes=64)
+            by_pair = grouped[:].rearrange("p x (w q j) -> p w x q j", w=PIXEL_PAIRS, j=PACK)
+            for pair in range(PIXEL_PAIRS):
+                bank = psum.tile([P, PACK, P], F32, tag="bank")
+                for j in range(PACK):
+                    nc.tensor.transpose(bank[:, j, :], words[:, j, pair, :], identity[:])
+                planes = bank[:].bitcast(BF16).rearrange("p j (x q) -> p x q j", x=WINDOWS_PER_GROUP)
+                copy = nc.scalar.copy if pair % 2 == 0 else nc.vector.tensor_copy
+                copy(out=by_pair[:, pair, 0:windows], in_=planes[:, 0:windows])
+            for x in range(windows):
+                c = first_window + x
+                nc.vector.quantize_mx(
+                    out=tub_codes[:, c, :].bitcast(E4M3_X4),
+                    scales=tub_scales[:, c, :],
+                    in_=grouped[:, x, :],
+                )
+
+        sums = [psum.tile([P, FEATURES], F32, name="sums%d" % m, tag="bank") for m in range(EMBED_TILES)]
+        half = EMBED // 2
+        for c in range(WINDOWS):
+            raw = grad_in.tile([P, PACK, EMBED], BF16)
+            nc.sync.dma_start(
+                out=raw[:].rearrange("p j e -> p (j e)"),
+                in_=grad_rows[c * WINDOW : (c + 1) * WINDOW, :].rearrange("(p j) e -> p (j e)", j=PACK),
+            )
+            side_by_side = grad_stage.tile([P, EMBED, PACK], BF16, align_bytes=64)
+            for h, copy in enumerate((nc.vector.tensor_copy, nc.scalar.copy)):
+                cols = slice(h * half, (h + 1) * half)
+                copy(
+                    out=side_by_side[:, cols, :].rearrange("p (g i) j -> p g j i", i=4),
+                    in_=raw[:, :, cols].rearrange("p j (g i) -> p g j i", i=4),
+                )
+            for h in range(2):
+                cols = slice(h * half, (h + 1) * half)
+                nc.vector.quantize_mx(
+                    out=grad_codes[:, c, cols].bitcast(E5M2_X4),
+                    scales=grad_scales[:, c, cols],
+                    in_=side_by_side[:, cols, :].rearrange("p e j -> p (e j)"),
+                )
+            for m in range(EMBED_TILES):
+                cols = slice(m * P, (m + 1) * P)
+                nc.tensor.matmul_mx(
+                    out=sums[m][:],
+                    lhsT=grad_codes[:, c, cols].bitcast(E5M2_X4),
+                    lhsT_scale=grad_scales[:, c, cols],
+                    rhs=tub_codes[:, c, :].bitcast(E4M3_X4),
+                    rhs_scale=tub_scales[:, c, :],
+                    start=(c == 0),
+                    stop=(c == WINDOWS - 1),
+                )
+
+        for m in range(EMBED_TILES):
+            result = results.tile([P, FEATURES], F32)
+            by_frame = sums[m][:].rearrange(
+                "p (w y s e) -> p s y w e", w=PIXEL_PAIRS, y=PATCH, s=FRAMES_PER_TUBE
+            )
+            copy = nc.vector.tensor_copy if m % 2 == 0 else nc.scalar.copy
+            for ts in range(FRAMES_PER_TUBE):
+                copy(
+                    out=result[:, ts * PATCH * PATCH : (ts + 1) * PATCH * PATCH].rearrange(
+                        "p (y w e) -> p y w e", y=PATCH, w=PIXEL_PAIRS
+                    ),
+                    in_=by_frame[:, ts],
+                )
+            nc.sync.dma_start(out=out[m * P : (m + 1) * P, :], in_=result[:])

@@ -28,7 +28,7 @@ FEATURES = FRAMES_PER_TUBE * PATCH * PATCH
 EMBED_TILES = EMBED // P
 
 WINDOWS_PER_GROUP = P // (PATCH * FRAMES_PER_TUBE)
-GROUPS = -(-WINDOWS // WINDOWS_PER_GROUP)
+GROUPS = ((0, 1, 2, 3), (8,), (4, 5, 6, 7))
 PIXEL_PAIRS = PATCH // 2
 LEAD_ROOM = TOKENS_PER_TUBE - PACK
 ROW_SLOTS = 16 * TOKENS_PER_TUBE
@@ -37,8 +37,7 @@ FLOPS = 2 * TOKENS * EMBED * FEATURES
 BYTES = 2 * TOKENS * FEATURES + 2 * TOKENS * EMBED + 4 * EMBED * FEATURES
 
 
-def load_window_rows(nc, video_rows, rows, c):
-    x = c % WINDOWS_PER_GROUP
+def load_window_rows(nc, video_rows, rows, c, x):
     first_tube = (c * WINDOW) // TOKENS_PER_TUBE
     last_tube = (c * WINDOW + WINDOW - 1) // TOKENS_PER_TUBE
     tubes = last_tube - first_tube + 1
@@ -67,30 +66,52 @@ def tile_tubeletembedding_kernel(tc, video, W, b, pos_embed, grad_out, out):
     with ExitStack() as stack:
         keep = stack.enter_context(tc.tile_pool(name="keep", bufs=1))
         stage = stack.enter_context(tc.tile_pool(name="stage", bufs=2))
-        grad_in = stack.enter_context(tc.tile_pool(name="grad_in", bufs=4))
-        grad_stage = stack.enter_context(tc.tile_pool(name="grad_stage", bufs=3))
+        grad_in = stack.enter_context(tc.tile_pool(name="grad_in", bufs=7))
+        grad_stage = stack.enter_context(tc.tile_pool(name="grad_stage", bufs=4))
+        grad_packed = stack.enter_context(tc.tile_pool(name="grad_packed", bufs=4))
         results = stack.enter_context(tc.tile_pool(name="results", bufs=4))
         psum = stack.enter_context(tc.psum_pool(name="psum", bufs=8))
 
         identity = keep.tile([P, P], F32)
         make_identity(nc, identity[:])
+        reorder = keep.tile([P, P], F32)
+        nc.vector.tensor_copy(
+            out=reorder[:].rearrange("p (x s y) -> p x s y", s=FRAMES_PER_TUBE, y=PATCH),
+            in_=identity[:].rearrange("p (x y s) -> p x s y", s=FRAMES_PER_TUBE, y=PATCH),
+        )
+
+        stack.enter_context(tc.manual_schedule())
 
         tub_codes = keep.tile([P, WINDOWS, FEATURES], U32, align_bytes=64)
         tub_scales = keep.tile([P, WINDOWS, FEATURES], U8, align_bytes=64)
-        grad_codes = keep.tile([P, WINDOWS, EMBED], U32, align_bytes=64)
-        grad_scales = keep.tile([P, WINDOWS, EMBED], U8, align_bytes=64)
 
-        rows_a = keep.tile([P, ROW_SLOTS * PATCH], BF16)
-        rows_b = keep.tile([P, ROW_SLOTS * PATCH], BF16)
-        rows_of_group = [rows_a, rows_b, rows_a]
+        rows_of_group = []
+        for g, group in enumerate(GROUPS):
+            rows = keep.tile([P, ROW_SLOTS * PATCH], BF16, name="rows%d" % g)
+            if len(group) < WINDOWS_PER_GROUP:
+                nc.gpsimd.memset(rows[:].bitcast(F32), 0.0)
+            for x, c in enumerate(group):
+                load_window_rows(nc, video_rows, rows, c, x)
+            rows_of_group.append(rows)
+        raw_of_window = []
+        for c in range(WINDOWS):
+            raw = grad_in.tile([P, PACK, EMBED], BF16, name="raw")
+            nc.sync.dma_start(
+                out=raw[:].rearrange("p j e -> p (j e)"),
+                in_=grad_rows[c * WINDOW : (c + 1) * WINDOW, :].rearrange("(p j) e -> p (j e)", j=PACK),
+            )
+            raw_of_window.append(raw)
 
-        for group in range(GROUPS):
-            rows = rows_of_group[group]
-            first_window = group * WINDOWS_PER_GROUP
-            windows = min(WINDOWS_PER_GROUP, WINDOWS - first_window)
-            for x in range(windows):
-                load_window_rows(nc, video_rows, rows, first_window + x)
+        def quantise_tubelets(c, grouped_window):
+            nc.vector.quantize_mx(
+                out=tub_codes[:, c, :].bitcast(E4M3_X4),
+                scales=tub_scales[:, c, :],
+                in_=grouped_window,
+            )
 
+        postponed = []
+        for group, rows in zip(GROUPS, rows_of_group):
+            windows = len(group)
             words = (
                 rows[:]
                 .bitcast(F32)[:, LEAD_ROOM * PIXEL_PAIRS : (LEAD_ROOM + WINDOW) * PIXEL_PAIRS]
@@ -101,63 +122,65 @@ def tile_tubeletembedding_kernel(tc, video, W, b, pos_embed, grad_out, out):
             for pair in range(PIXEL_PAIRS):
                 bank = psum.tile([P, PACK, P], F32, tag="bank")
                 for j in range(PACK):
-                    nc.tensor.transpose(bank[:, j, :], words[:, j, pair, :], identity[:])
+                    nc.tensor.transpose(bank[:, j, :], words[:, j, pair, :], reorder[:])
                 planes = bank[:].bitcast(BF16).rearrange("p j (x q) -> p x q j", x=WINDOWS_PER_GROUP)
                 copy = nc.scalar.copy if pair % 2 == 0 else nc.vector.tensor_copy
                 copy(out=by_pair[:, pair, 0:windows], in_=planes[:, 0:windows])
-            for x in range(windows):
-                c = first_window + x
-                nc.vector.quantize_mx(
-                    out=tub_codes[:, c, :].bitcast(E4M3_X4),
-                    scales=tub_scales[:, c, :],
-                    in_=grouped[:, x, :],
-                )
+            for x, c in enumerate(group):
+                if group is GROUPS[-1]:
+                    postponed.append((c, grouped[:, x, :]))
+                else:
+                    quantise_tubelets(c, grouped[:, x, :])
 
         sums = [psum.tile([P, FEATURES], F32, name="sums%d" % m, tag="bank") for m in range(EMBED_TILES)]
         half = EMBED // 2
-        for c in range(WINDOWS):
-            raw = grad_in.tile([P, PACK, EMBED], BF16)
-            nc.sync.dma_start(
-                out=raw[:].rearrange("p j e -> p (j e)"),
-                in_=grad_rows[c * WINDOW : (c + 1) * WINDOW, :].rearrange("(p j) e -> p (j e)", j=PACK),
-            )
-            side_by_side = grad_stage.tile([P, EMBED, PACK], BF16, align_bytes=64)
-            for h, copy in enumerate((nc.vector.tensor_copy, nc.scalar.copy)):
-                cols = slice(h * half, (h + 1) * half)
+        halves = (slice(0, half), slice(half, EMBED))
+
+        def regroup(c):
+            raw = raw_of_window[c]
+            side_by_side = grad_stage.tile([P, EMBED, PACK], BF16, name="side_by_side", align_bytes=64)
+            for cols, copy in zip(halves, (nc.vector.tensor_copy, nc.scalar.copy)):
                 copy(
                     out=side_by_side[:, cols, :].rearrange("p (g i) j -> p g j i", i=4),
                     in_=raw[:, :, cols].rearrange("p j (g i) -> p g j i", i=4),
                 )
-            for h in range(2):
-                cols = slice(h * half, (h + 1) * half)
-                nc.vector.quantize_mx(
-                    out=grad_codes[:, c, cols].bitcast(E5M2_X4),
-                    scales=grad_scales[:, c, cols],
-                    in_=side_by_side[:, cols, :].rearrange("p e j -> p (e j)"),
-                )
+            return side_by_side
+
+        def quantise_half(h, side_by_side, grad_codes, grad_scales):
+            cols = halves[h]
+            nc.vector.quantize_mx(
+                out=grad_codes[:, cols].bitcast(E5M2_X4),
+                scales=grad_scales[:, cols],
+                in_=side_by_side[:, cols, :].rearrange("p e j -> p (e j)"),
+            )
+
+        regrouped = regroup(0)
+        for c in range(WINDOWS):
+            grad_codes = grad_packed.tile([P, EMBED], U32, align_bytes=64)
+            grad_scales = grad_packed.tile([P, EMBED], U8, align_bytes=64)
+            quantise_half(0, regrouped, grad_codes, grad_scales)
+            following = regroup(c + 1) if c + 1 < WINDOWS else None
+            quantise_half(1, regrouped, grad_codes, grad_scales)
+            if c < len(postponed):
+                quantise_tubelets(*postponed[c])
             for m in range(EMBED_TILES):
                 cols = slice(m * P, (m + 1) * P)
                 nc.tensor.matmul_mx(
                     out=sums[m][:],
-                    lhsT=grad_codes[:, c, cols].bitcast(E5M2_X4),
-                    lhsT_scale=grad_scales[:, c, cols],
+                    lhsT=grad_codes[:, cols].bitcast(E5M2_X4),
+                    lhsT_scale=grad_scales[:, cols],
                     rhs=tub_codes[:, c, :].bitcast(E4M3_X4),
                     rhs_scale=tub_scales[:, c, :],
                     start=(c == 0),
                     stop=(c == WINDOWS - 1),
                 )
+            regrouped = following
 
         for m in range(EMBED_TILES):
             result = results.tile([P, FEATURES], F32)
-            by_frame = sums[m][:].rearrange(
-                "p (w y s e) -> p s y w e", w=PIXEL_PAIRS, y=PATCH, s=FRAMES_PER_TUBE
-            )
             copy = nc.vector.tensor_copy if m % 2 == 0 else nc.scalar.copy
-            for ts in range(FRAMES_PER_TUBE):
-                copy(
-                    out=result[:, ts * PATCH * PATCH : (ts + 1) * PATCH * PATCH].rearrange(
-                        "p (y w e) -> p y w e", y=PATCH, w=PIXEL_PAIRS
-                    ),
-                    in_=by_frame[:, ts],
-                )
+            copy(
+                out=result[:].rearrange("p (r w e) -> p r w e", w=PIXEL_PAIRS, e=2),
+                in_=sums[m][:].rearrange("p (w r e) -> p r w e", w=PIXEL_PAIRS, e=2),
+            )
             nc.sync.dma_start(out=out[m * P : (m + 1) * P, :], in_=result[:])

@@ -15,122 +15,137 @@ PACK = 4
 WINDOW = P * PACK
 
 BATCH = 16
-TUBES = 128
-FRAMES_PER_TUBE = 2
+TUBES = 8
+FRAMES = 2
 GRID = 6
 PATCH = 16
-IMAGE_ROW = GRID * PATCH
-TOKENS_PER_TUBE = GRID * GRID
-TOKENS = TUBES * TOKENS_PER_TUBE
+GRID_ROW = PATCH * GRID * PATCH
+STRIP = 2 * GRID_ROW
+STRIP_TOKENS = 2 * GRID
+STRIPS_PER_FRAME = GRID // 2
+LOADS = BATCH // 2
+LOAD_TUBES = 2 * TUBES
+STRIPS = LOAD_TUBES * FRAMES * STRIPS_PER_FRAME
+LOAD_TOKENS = LOAD_TUBES * GRID * GRID
+TOKENS = LOADS * LOAD_TOKENS
 WINDOWS = TOKENS // WINDOW
 EMBED = 1024
-FEATURES = FRAMES_PER_TUBE * PATCH * PATCH
+FRAME_FEATURES = PATCH * PATCH
+FEATURES = FRAMES * FRAME_FEATURES
 EMBED_TILES = EMBED // P
-
-WINDOWS_PER_GROUP = P // (PATCH * FRAMES_PER_TUBE)
-GROUPS = ((0, 1, 2, 3), (8,), (4, 5, 6, 7))
-PIXEL_PAIRS = PATCH // 2
-LEAD_ROOM = TOKENS_PER_TUBE - PACK
-ROW_SLOTS = 16 * TOKENS_PER_TUBE
 
 FLOPS = 2 * TOKENS * EMBED * FEATURES
 BYTES = 2 * TOKENS * FEATURES + 2 * TOKENS * EMBED + 4 * EMBED * FEATURES
 
 
-def load_window_rows(nc, video_rows, rows, c, x):
-    first_tube = (c * WINDOW) // TOKENS_PER_TUBE
-    last_tube = (c * WINDOW + WINDOW - 1) // TOKENS_PER_TUBE
-    tubes = last_tube - first_tube + 1
-    lead = c * WINDOW - first_tube * TOKENS_PER_TUBE
-    start = (LEAD_ROOM - lead) * PATCH
-    for i in range(GRID):
-        for ts in range(FRAMES_PER_TUBE):
-            base = x * PATCH * FRAMES_PER_TUBE
-            mine = rows[base + ts : base + PATCH * FRAMES_PER_TUBE : FRAMES_PER_TUBE, :]
-            by_tube = mine[:, start : start + tubes * TOKENS_PER_TUBE * PATCH].rearrange(
-                "y (t r) -> y t r", t=tubes
-            )
-            nc.sync.dma_start(
-                out=by_tube[:, :, i * IMAGE_ROW : (i + 1) * IMAGE_ROW],
-                in_=video_rows[ts, i, :, first_tube : last_tube + 1, :],
-            )
-
-
 def tile_tubeletembedding_kernel(tc, video, W, b, pos_embed, grad_out, out):
     nc = tc.nc
-    video_rows = video.rearrange("b f c h w -> (b f c h) w").rearrange(
-        "(t s i y) w -> s i y t w", s=FRAMES_PER_TUBE, i=GRID, y=PATCH
-    )
+    strips = video.rearrange("b f c h w -> (b f c h w)").rearrange("(g p x) -> p g x", p=STRIPS, x=STRIP)
     grad_rows = grad_out.rearrange("b n e -> (b n) e")
 
     with ExitStack() as stack:
         keep = stack.enter_context(tc.tile_pool(name="keep", bufs=1))
-        stage = stack.enter_context(tc.tile_pool(name="stage", bufs=2))
-        grad_in = stack.enter_context(tc.tile_pool(name="grad_in", bufs=7))
-        grad_stage = stack.enter_context(tc.tile_pool(name="grad_stage", bufs=4))
-        grad_packed = stack.enter_context(tc.tile_pool(name="grad_packed", bufs=4))
-        results = stack.enter_context(tc.tile_pool(name="results", bufs=4))
+        stage = stack.enter_context(tc.tile_pool(name="stage", bufs=3))
+        grad_in = stack.enter_context(tc.tile_pool(name="grad_in", bufs=5))
+        grad_stage = stack.enter_context(tc.tile_pool(name="grad_stage", bufs=3))
+        grad_packed = stack.enter_context(tc.tile_pool(name="grad_packed", bufs=3))
+        results = stack.enter_context(tc.tile_pool(name="results", bufs=3))
         psum = stack.enter_context(tc.psum_pool(name="psum", bufs=8))
 
         identity = keep.tile([P, P], F32)
         make_identity(nc, identity[:])
-        reorder = keep.tile([P, P], F32)
+        by_frame = keep.tile([P, P], F32)
+        nc.vector.tensor_copy(out=by_frame[:, STRIPS:P], in_=identity[:, STRIPS:P])
         nc.vector.tensor_copy(
-            out=reorder[:].rearrange("p (x s y) -> p x s y", s=FRAMES_PER_TUBE, y=PATCH),
-            in_=identity[:].rearrange("p (x y s) -> p x s y", s=FRAMES_PER_TUBE, y=PATCH),
+            out=by_frame[:, 0:STRIPS].rearrange("p (s a i) -> p s a i", s=FRAMES, i=STRIPS_PER_FRAME),
+            in_=identity[:, 0:STRIPS].rearrange("p (a s i) -> p s a i", s=FRAMES, i=STRIPS_PER_FRAME),
         )
 
-        stack.enter_context(tc.manual_schedule())
-
-        tub_codes = keep.tile([P, WINDOWS, FEATURES], U32, align_bytes=64)
-        tub_scales = keep.tile([P, WINDOWS, FEATURES], U8, align_bytes=64)
-
-        rows_of_group = []
-        for g, group in enumerate(GROUPS):
-            rows = keep.tile([P, ROW_SLOTS * PATCH], BF16, name="rows%d" % g)
-            if len(group) < WINDOWS_PER_GROUP:
-                nc.gpsimd.memset(rows[:].bitcast(F32), 0.0)
-            for x, c in enumerate(group):
-                load_window_rows(nc, video_rows, rows, c, x)
-            rows_of_group.append(rows)
+        as_it_lies = keep.tile([P, LOADS, STRIP], BF16)
+        for g in range(LOADS):
+            nc.sync.dma_start(out=as_it_lies[0:STRIPS, g, :], in_=strips[:, g, :])
         raw_of_window = []
         for c in range(WINDOWS):
             raw = grad_in.tile([P, PACK, EMBED], BF16, name="raw")
             nc.sync.dma_start(
-                out=raw[:].rearrange("p j e -> p (j e)"),
-                in_=grad_rows[c * WINDOW : (c + 1) * WINDOW, :].rearrange("(p j) e -> p (j e)", j=PACK),
+                out=raw[:].rearrange("p u e -> p (u e)"),
+                in_=grad_rows[c * WINDOW : (c + 1) * WINDOW, :].rearrange("(p u) e -> p (u e)", u=PACK),
             )
             raw_of_window.append(raw)
 
-        def quantise_tubelets(c, grouped_window):
+        sorted_tiles = []
+        for n in range(3):
+            sorted_strips = keep.tile([P, STRIP_TOKENS, FRAME_FEATURES], BF16, name="sorted%d" % n)
+            nc.vector.memset(sorted_strips[STRIPS:P].bitcast(mybir.dt.int32), 0)
+            sorted_tiles.append(sorted_strips)
+
+        by_feature = keep.tile([P, FRAMES, TOKENS], F32)
+        tub_codes = keep.tile([P, WINDOWS, FEATURES], U32, align_bytes=64)
+        tub_scales = keep.tile([P, WINDOWS, FEATURES], U8, align_bytes=64)
+
+        def sort(g):
+            sorted_strips = sorted_tiles[g % len(sorted_tiles)]
+            for row in range(2):
+                nc.vector.tensor_copy(
+                    out=sorted_strips[0:STRIPS, row * GRID : (row + 1) * GRID, :].rearrange(
+                        "p j (y x) -> p j y x", x=PATCH
+                    ),
+                    in_=as_it_lies[0:STRIPS, g, row * GRID_ROW : (row + 1) * GRID_ROW].rearrange(
+                        "p (y j x) -> p j y x", j=GRID, x=PATCH
+                    ),
+                )
+
+        def first_turn(g):
+            words = sorted_tiles[g % len(sorted_tiles)][:].bitcast(F32)
+            landing = by_feature[:, :, g * LOAD_TOKENS : (g + 1) * LOAD_TOKENS].rearrange(
+                "p s (r q u) -> p q s r u", q=STRIP_TOKENS // PACK, u=PACK
+            )
+            for q in range(STRIP_TOKENS // PACK):
+                bank = psum.tile([P, PACK, P], F32, tag="bank")
+                for u in range(PACK):
+                    nc.tensor.transpose(bank[:, u, :], words[:, q * PACK + u, :], by_frame[:])
+                nc.scalar.copy(
+                    out=landing[:, q],
+                    in_=bank[:, :, 0:STRIPS].rearrange("p u (s r) -> p s r u", s=FRAMES),
+                )
+
+        def second_turn(c):
+            grouped = stage.tile([P, FEATURES * PACK], BF16, name="grouped", align_bytes=64)
+            for ts, copy in enumerate((nc.scalar.copy, nc.vector.tensor_copy)):
+                window = by_feature[:, ts, c * WINDOW : (c + 1) * WINDOW].rearrange("p (m u) -> p u m", u=PACK)
+                bank = psum.tile([P, PACK, P], F32, tag="bank")
+                for u in range(PACK):
+                    nc.tensor.transpose(bank[:, u, :], window[:, u, :], identity[:])
+                frame_cols = slice(ts * FRAME_FEATURES * PACK, (ts + 1) * FRAME_FEATURES * PACK)
+                copy(
+                    out=grouped[:, frame_cols].rearrange("p (q u) -> p q u", u=PACK),
+                    in_=bank[:].bitcast(BF16).rearrange("p u q -> p q u"),
+                )
+            return grouped
+
+        def quantise_tubelets(c, grouped):
             nc.vector.quantize_mx(
                 out=tub_codes[:, c, :].bitcast(E4M3_X4),
                 scales=tub_scales[:, c, :],
-                in_=grouped_window,
+                in_=grouped[:],
             )
 
-        postponed = []
-        for group, rows in zip(GROUPS, rows_of_group):
-            windows = len(group)
-            words = (
-                rows[:]
-                .bitcast(F32)[:, LEAD_ROOM * PIXEL_PAIRS : (LEAD_ROOM + WINDOW) * PIXEL_PAIRS]
-                .rearrange("p (m j w) -> p j w m", j=PACK, w=PIXEL_PAIRS)
-            )
-            grouped = stage.tile([P, WINDOWS_PER_GROUP, FEATURES * PACK], BF16, align_bytes=64)
-            by_pair = grouped[:].rearrange("p x (w q j) -> p w x q j", w=PIXEL_PAIRS, j=PACK)
-            for pair in range(PIXEL_PAIRS):
-                bank = psum.tile([P, PACK, P], F32, tag="bank")
-                for j in range(PACK):
-                    nc.tensor.transpose(bank[:, j, :], words[:, j, pair, :], reorder[:])
-                planes = bank[:].bitcast(BF16).rearrange("p j (x q) -> p x q j", x=WINDOWS_PER_GROUP)
-                copy = nc.scalar.copy if pair % 2 == 0 else nc.vector.tensor_copy
-                copy(out=by_pair[:, pair, 0:windows], in_=planes[:, 0:windows])
-            for x, c in enumerate(group):
-                if group is GROUPS[-1]:
-                    postponed.append((c, grouped[:, x, :]))
-                else:
-                    quantise_tubelets(c, grouped[:, x, :])
+        stack.enter_context(tc.manual_schedule())
+        turned = []
+        quantised = 0
+        sort(0)
+        first_turn(0)
+        sort(1)
+        for g in range(LOADS):
+            if g + 1 < LOADS:
+                first_turn(g + 1)
+            if g + 2 < LOADS:
+                sort(g + 2)
+            while len(turned) < WINDOWS and (len(turned) + 1) * WINDOW <= (g + 1) * LOAD_TOKENS:
+                turned.append(second_turn(len(turned)))
+                if len(turned) - quantised > 1:
+                    quantise_tubelets(quantised, turned[quantised])
+                    quantised += 1
 
         sums = [psum.tile([P, FEATURES], F32, name="sums%d" % m, tag="bank") for m in range(EMBED_TILES)]
         half = EMBED // 2
@@ -141,8 +156,8 @@ def tile_tubeletembedding_kernel(tc, video, W, b, pos_embed, grad_out, out):
             side_by_side = grad_stage.tile([P, EMBED, PACK], BF16, name="side_by_side", align_bytes=64)
             for cols, copy in zip(halves, (nc.vector.tensor_copy, nc.scalar.copy)):
                 copy(
-                    out=side_by_side[:, cols, :].rearrange("p (g i) j -> p g j i", i=4),
-                    in_=raw[:, :, cols].rearrange("p j (g i) -> p g j i", i=4),
+                    out=side_by_side[:, cols, :].rearrange("p (g r) u -> p g u r", r=4),
+                    in_=raw[:, :, cols].rearrange("p u (g r) -> p g u r", r=4),
                 )
             return side_by_side
 
@@ -151,7 +166,7 @@ def tile_tubeletembedding_kernel(tc, video, W, b, pos_embed, grad_out, out):
             nc.vector.quantize_mx(
                 out=grad_codes[:, cols].bitcast(E5M2_X4),
                 scales=grad_scales[:, cols],
-                in_=side_by_side[:, cols, :].rearrange("p e j -> p (e j)"),
+                in_=side_by_side[:, cols, :].rearrange("p e u -> p (e u)"),
             )
 
         regrouped = regroup(0)
@@ -161,8 +176,9 @@ def tile_tubeletembedding_kernel(tc, video, W, b, pos_embed, grad_out, out):
             quantise_half(0, regrouped, grad_codes, grad_scales)
             following = regroup(c + 1) if c + 1 < WINDOWS else None
             quantise_half(1, regrouped, grad_codes, grad_scales)
-            if c < len(postponed):
-                quantise_tubelets(*postponed[c])
+            if quantised < WINDOWS:
+                quantise_tubelets(quantised, turned[quantised])
+                quantised += 1
             for m in range(EMBED_TILES):
                 cols = slice(m * P, (m + 1) * P)
                 nc.tensor.matmul_mx(
@@ -179,8 +195,5 @@ def tile_tubeletembedding_kernel(tc, video, W, b, pos_embed, grad_out, out):
         for m in range(EMBED_TILES):
             result = results.tile([P, FEATURES], F32)
             copy = nc.vector.tensor_copy if m % 2 == 0 else nc.scalar.copy
-            copy(
-                out=result[:].rearrange("p (r w e) -> p r w e", w=PIXEL_PAIRS, e=2),
-                in_=sums[m][:].rearrange("p (w r e) -> p r w e", w=PIXEL_PAIRS, e=2),
-            )
+            copy(out=result[:], in_=sums[m][:])
             nc.sync.dma_start(out=out[m * P : (m + 1) * P, :], in_=result[:])

@@ -111,12 +111,13 @@ def tile_tubeletembedding_kernel(tc, video, W, b, pos_embed, grad_out, out):
 
         def second_turn(c):
             grouped = stage.tile([P, FEATURES * PACK], BF16, name="grouped", align_bytes=64)
-            for ts, copy in enumerate((nc.scalar.copy, nc.vector.tensor_copy)):
+            for ts in range(FRAMES):
                 window = by_feature[:, ts, c * WINDOW : (c + 1) * WINDOW].rearrange("p (m u) -> p u m", u=PACK)
                 bank = psum.tile([P, PACK, P], F32, tag="bank")
                 for u in range(PACK):
                     nc.tensor.transpose(bank[:, u, :], window[:, u, :], identity[:])
                 frame_cols = slice(ts * FRAME_FEATURES * PACK, (ts + 1) * FRAME_FEATURES * PACK)
+                copy = nc.vector.tensor_copy if (c * FRAMES + ts) % 3 == 1 else nc.scalar.copy
                 copy(
                     out=grouped[:, frame_cols].rearrange("p (q u) -> p q u", u=PACK),
                     in_=bank[:].bitcast(BF16).rearrange("p u q -> p q u"),

@@ -46,10 +46,10 @@ def tile_tubeletembedding_kernel(tc, video, W, b, pos_embed, grad_out, out):
     with ExitStack() as stack:
         keep = stack.enter_context(tc.tile_pool(name="keep", bufs=1))
         stage = stack.enter_context(tc.tile_pool(name="stage", bufs=3))
-        grad_in = stack.enter_context(tc.tile_pool(name="grad_in", bufs=5))
+        grad_in = stack.enter_context(tc.tile_pool(name="grad_in", bufs=4))
         grad_stage = stack.enter_context(tc.tile_pool(name="grad_stage", bufs=3))
         grad_packed = stack.enter_context(tc.tile_pool(name="grad_packed", bufs=3))
-        results = stack.enter_context(tc.tile_pool(name="results", bufs=3))
+        results = stack.enter_context(tc.tile_pool(name="results", bufs=EMBED_TILES))
         psum = stack.enter_context(tc.psum_pool(name="psum", bufs=8))
 
         identity = keep.tile([P, P], F32)
@@ -131,6 +131,34 @@ def tile_tubeletembedding_kernel(tc, video, W, b, pos_embed, grad_out, out):
                 in_=grouped[:],
             )
 
+        half = EMBED // 2
+        halves = (slice(0, half), slice(half, EMBED))
+        regrouped = []
+        packed = []
+
+        def regroup(c):
+            raw = raw_of_window[c]
+            side_by_side = grad_stage.tile([P, EMBED, PACK], BF16, name="side_by_side", align_bytes=64)
+            for cols, copy in zip(halves, (nc.vector.tensor_copy, nc.scalar.copy)):
+                copy(
+                    out=side_by_side[:, cols, :].rearrange("p (g r) u -> p g u r", r=4),
+                    in_=raw[:, :, cols].rearrange("p u (g r) -> p g u r", r=4),
+                )
+            regrouped.append(side_by_side)
+
+        def prepare(c):
+            grad_codes = grad_packed.tile([P, EMBED], U32, name="grad_codes", align_bytes=64)
+            grad_scales = grad_packed.tile([P, EMBED], U8, name="grad_scales", align_bytes=64)
+            for h, cols in enumerate(halves):
+                nc.vector.quantize_mx(
+                    out=grad_codes[:, cols].bitcast(E5M2_X4),
+                    scales=grad_scales[:, cols],
+                    in_=regrouped[c][:, cols, :].rearrange("p e u -> p (e u)"),
+                )
+                if h == 0 and c + 1 < WINDOWS:
+                    regroup(c + 1)
+            packed.append((grad_codes, grad_scales))
+
         stack.enter_context(tc.manual_schedule())
         turned = []
         quantised = 0
@@ -147,39 +175,19 @@ def tile_tubeletembedding_kernel(tc, video, W, b, pos_embed, grad_out, out):
                 if len(turned) - quantised > 1:
                     quantise_tubelets(quantised, turned[quantised])
                     quantised += 1
+            if g == LOADS - 3:
+                regroup(0)
+            if g == LOADS - 2:
+                prepare(0)
 
         sums = [psum.tile([P, FEATURES], F32, name="sums%d" % m, tag="bank") for m in range(EMBED_TILES)]
-        half = EMBED // 2
-        halves = (slice(0, half), slice(half, EMBED))
-
-        def regroup(c):
-            raw = raw_of_window[c]
-            side_by_side = grad_stage.tile([P, EMBED, PACK], BF16, name="side_by_side", align_bytes=64)
-            for cols, copy in zip(halves, (nc.vector.tensor_copy, nc.scalar.copy)):
-                copy(
-                    out=side_by_side[:, cols, :].rearrange("p (g r) u -> p g u r", r=4),
-                    in_=raw[:, :, cols].rearrange("p u (g r) -> p g u r", r=4),
-                )
-            return side_by_side
-
-        def quantise_half(h, side_by_side, grad_codes, grad_scales):
-            cols = halves[h]
-            nc.vector.quantize_mx(
-                out=grad_codes[:, cols].bitcast(E5M2_X4),
-                scales=grad_scales[:, cols],
-                in_=side_by_side[:, cols, :].rearrange("p e u -> p (e u)"),
-            )
-
-        regrouped = regroup(0)
         for c in range(WINDOWS):
-            grad_codes = grad_packed.tile([P, EMBED], U32, align_bytes=64)
-            grad_scales = grad_packed.tile([P, EMBED], U8, align_bytes=64)
-            quantise_half(0, regrouped, grad_codes, grad_scales)
-            following = regroup(c + 1) if c + 1 < WINDOWS else None
-            quantise_half(1, regrouped, grad_codes, grad_scales)
+            if c + 1 < WINDOWS:
+                prepare(c + 1)
             if quantised < WINDOWS:
                 quantise_tubelets(quantised, turned[quantised])
                 quantised += 1
+            grad_codes, grad_scales = packed[c]
             for m in range(EMBED_TILES):
                 cols = slice(m * P, (m + 1) * P)
                 nc.tensor.matmul_mx(
@@ -191,7 +199,6 @@ def tile_tubeletembedding_kernel(tc, video, W, b, pos_embed, grad_out, out):
                     start=(c == 0),
                     stop=(c == WINDOWS - 1),
                 )
-            regrouped = following
 
         for m in range(EMBED_TILES):
             result = results.tile([P, FEATURES], F32)

@@ -62,8 +62,14 @@ def tile_tubeletembedding_kernel(tc, video, W, b, pos_embed, grad_out, out):
         )
 
         as_it_lies = keep.tile([P, LOADS, STRIP], BF16)
-        for g in range(LOADS):
-            nc.sync.dma_start(out=as_it_lies[0:STRIPS, g, :], in_=strips[:, g, :])
+        all_strips = video.rearrange("b f c h w -> (b f c h w)").rearrange("(s x) -> s x", x=STRIP)
+        for row in range(2):
+            cols = slice(row * GRID_ROW, (row + 1) * GRID_ROW)
+            nc.sync.dma_start(out=as_it_lies[:, 0, cols], in_=all_strips[0:P, cols])
+        for g in range(1, LOADS - 1):
+            nc.sync.dma_start(out=as_it_lies[:, g, :], in_=all_strips[g * STRIPS : g * STRIPS + P, :])
+        nc.sync.dma_start(out=as_it_lies[0:STRIPS, LOADS - 1, :], in_=strips[:, LOADS - 1, :])
+        nc.sync.dma_start(out=as_it_lies[STRIPS:P, LOADS - 1, :], in_=all_strips[0 : P - STRIPS, :])
         raw_of_window = []
         for c in range(WINDOWS):
             raw = grad_in.tile([P, PACK, EMBED], BF16, name="raw")
@@ -76,7 +82,6 @@ def tile_tubeletembedding_kernel(tc, video, W, b, pos_embed, grad_out, out):
         sorted_tiles = []
         for n in range(3):
             sorted_strips = keep.tile([P, STRIP_TOKENS, FRAME_FEATURES], BF16, name="sorted%d" % n)
-            nc.vector.memset(sorted_strips[STRIPS:P].bitcast(mybir.dt.int32), 0)
             sorted_tiles.append(sorted_strips)
 
         by_feature = keep.tile([P, FRAMES, TOKENS], F32)
@@ -87,10 +92,10 @@ def tile_tubeletembedding_kernel(tc, video, W, b, pos_embed, grad_out, out):
             sorted_strips = sorted_tiles[g % len(sorted_tiles)]
             for row in range(2):
                 nc.vector.tensor_copy(
-                    out=sorted_strips[0:STRIPS, row * GRID : (row + 1) * GRID, :].rearrange(
+                    out=sorted_strips[:, row * GRID : (row + 1) * GRID, :].rearrange(
                         "p j (y x) -> p j y x", x=PATCH
                     ),
-                    in_=as_it_lies[0:STRIPS, g, row * GRID_ROW : (row + 1) * GRID_ROW].rearrange(
+                    in_=as_it_lies[:, g, row * GRID_ROW : (row + 1) * GRID_ROW].rearrange(
                         "p (y j x) -> p j y x", j=GRID, x=PATCH
                     ),
                 )
@@ -104,7 +109,8 @@ def tile_tubeletembedding_kernel(tc, video, W, b, pos_embed, grad_out, out):
                 bank = psum.tile([P, PACK, P], F32, tag="bank")
                 for u in range(PACK):
                     nc.tensor.transpose(bank[:, u, :], words[:, q * PACK + u, :], by_frame[:])
-                nc.scalar.copy(
+                copy = nc.vector.tensor_copy if g == 0 and q == 0 else nc.scalar.copy
+                copy(
                     out=landing[:, q],
                     in_=bank[:, :, 0:STRIPS].rearrange("p u (s r) -> p s r u", s=FRAMES),
                 )
@@ -117,7 +123,7 @@ def tile_tubeletembedding_kernel(tc, video, W, b, pos_embed, grad_out, out):
                 for u in range(PACK):
                     nc.tensor.transpose(bank[:, u, :], window[:, u, :], identity[:])
                 frame_cols = slice(ts * FRAME_FEATURES * PACK, (ts + 1) * FRAME_FEATURES * PACK)
-                copy = nc.vector.tensor_copy if (c * FRAMES + ts) % 3 == 1 else nc.scalar.copy
+                copy = nc.vector.tensor_copy if (c * FRAMES + ts) % 5 in (1, 3) else nc.scalar.copy
                 copy(
                     out=grouped[:, frame_cols].rearrange("p (q u) -> p q u", u=PACK),
                     in_=bank[:].bitcast(BF16).rearrange("p u q -> p q u"),

@@ -55,11 +55,6 @@ def tile_tubeletembedding_kernel(tc, video, W, b, pos_embed, grad_out, out):
         identity = keep.tile([P, P], F32)
         make_identity(nc, identity[:])
         by_frame = keep.tile([P, P], F32)
-        nc.vector.tensor_copy(out=by_frame[:, STRIPS:P], in_=identity[:, STRIPS:P])
-        nc.vector.tensor_copy(
-            out=by_frame[:, 0:STRIPS].rearrange("p (s a i) -> p s a i", s=FRAMES, i=STRIPS_PER_FRAME),
-            in_=identity[:, 0:STRIPS].rearrange("p (a s i) -> p s a i", s=FRAMES, i=STRIPS_PER_FRAME),
-        )
 
         as_it_lies = keep.tile([P, LOADS, STRIP], BF16)
         all_strips = video.rearrange("b f c h w -> (b f c h w)").rearrange("(s x) -> s x", x=STRIP)
@@ -109,8 +104,7 @@ def tile_tubeletembedding_kernel(tc, video, W, b, pos_embed, grad_out, out):
                 bank = psum.tile([P, PACK, P], F32, tag="bank")
                 for u in range(PACK):
                     nc.tensor.transpose(bank[:, u, :], words[:, q * PACK + u, :], by_frame[:])
-                copy = nc.vector.tensor_copy if g == 0 and q == 0 else nc.scalar.copy
-                copy(
+                nc.scalar.copy(
                     out=landing[:, q],
                     in_=bank[:, :, 0:STRIPS].rearrange("p u (s r) -> p s r u", s=FRAMES),
                 )
@@ -123,7 +117,7 @@ def tile_tubeletembedding_kernel(tc, video, W, b, pos_embed, grad_out, out):
                 for u in range(PACK):
                     nc.tensor.transpose(bank[:, u, :], window[:, u, :], identity[:])
                 frame_cols = slice(ts * FRAME_FEATURES * PACK, (ts + 1) * FRAME_FEATURES * PACK)
-                copy = nc.vector.tensor_copy if (c * FRAMES + ts) % 5 in (1, 3) else nc.scalar.copy
+                copy = nc.vector.tensor_copy if ts == 1 else nc.scalar.copy
                 copy(
                     out=grouped[:, frame_cols].rearrange("p (q u) -> p q u", u=PACK),
                     in_=bank[:].bitcast(BF16).rearrange("p u q -> p q u"),
@@ -145,7 +139,12 @@ def tile_tubeletembedding_kernel(tc, video, W, b, pos_embed, grad_out, out):
         def regroup(c):
             raw = raw_of_window[c]
             side_by_side = grad_stage.tile([P, EMBED, PACK], BF16, name="side_by_side", align_bytes=64)
-            for cols, copy in zip(halves, (nc.vector.tensor_copy, nc.scalar.copy)):
+            vector_cols = {WINDOWS - 2: 432, WINDOWS - 1: 304}.get(c, 464)
+            for cols, copy in (
+                (slice(0, vector_cols), nc.vector.tensor_copy),
+                (slice(vector_cols, half), nc.scalar.copy),
+                (slice(half, EMBED), nc.scalar.copy),
+            ):
                 copy(
                     out=side_by_side[:, cols, :].rearrange("p (g r) u -> p g u r", r=4),
                     in_=raw[:, :, cols].rearrange("p u (g r) -> p g u r", r=4),
@@ -166,6 +165,11 @@ def tile_tubeletembedding_kernel(tc, video, W, b, pos_embed, grad_out, out):
             packed.append((grad_codes, grad_scales))
 
         stack.enter_context(tc.manual_schedule())
+        nc.vector.tensor_copy(out=by_frame[:, STRIPS:P], in_=identity[:, STRIPS:P])
+        nc.vector.tensor_copy(
+            out=by_frame[:, 0:STRIPS].rearrange("p (s a i) -> p s a i", s=FRAMES, i=STRIPS_PER_FRAME),
+            in_=identity[:, 0:STRIPS].rearrange("p (a s i) -> p s a i", s=FRAMES, i=STRIPS_PER_FRAME),
+        )
         turned = []
         quantised = 0
         sort(0)

from contextlib import ExitStack

import concourse.mybir as mybir
from concourse.masks import make_identity

BF16 = mybir.dt.bfloat16
F32 = mybir.dt.float32
U32 = mybir.dt.uint32
U8 = mybir.dt.uint8
E4M3_X4 = mybir.dt.float8_e4m3fn_x4
E5M2_X4 = mybir.dt.float8_e5m2_x4

P = 128
PACK = 4
WINDOW = P * PACK

BATCH = 16
TUBES = 8
FRAMES = 2
GRID = 6
PATCH = 16
GRID_ROW = PATCH * GRID * PATCH
STRIP = 2 * GRID_ROW
STRIP_TOKENS = 2 * GRID
STRIPS_PER_FRAME = GRID // 2
LOADS = BATCH // 2
LOAD_TUBES = 2 * TUBES
STRIPS = LOAD_TUBES * FRAMES * STRIPS_PER_FRAME
LOAD_TOKENS = LOAD_TUBES * GRID * GRID
TOKENS = LOADS * LOAD_TOKENS
WINDOWS = TOKENS // WINDOW
EMBED = 1024
FRAME_FEATURES = PATCH * PATCH
FEATURES = FRAMES * FRAME_FEATURES
EMBED_TILES = EMBED // P

FLOPS = 2 * TOKENS * EMBED * FEATURES
BYTES = 2 * TOKENS * FEATURES + 2 * TOKENS * EMBED + 4 * EMBED * FEATURES


def tile_tubeletembedding_kernel(tc, video, W, b, pos_embed, grad_out, out):
    nc = tc.nc
    strips = video.rearrange("b f c h w -> (b f c h w)").rearrange("(g p x) -> p g x", p=STRIPS, x=STRIP)
    grad_rows = grad_out.rearrange("b n e -> (b n) e")

    with ExitStack() as stack:
        keep = stack.enter_context(tc.tile_pool(name="keep", bufs=1))
        stage = stack.enter_context(tc.tile_pool(name="stage", bufs=3))
        grad_in = stack.enter_context(tc.tile_pool(name="grad_in", bufs=4))
        grad_stage = stack.enter_context(tc.tile_pool(name="grad_stage", bufs=3))
        grad_packed = stack.enter_context(tc.tile_pool(name="grad_packed", bufs=3))
        results = stack.enter_context(tc.tile_pool(name="results", bufs=EMBED_TILES))
        psum = stack.enter_context(tc.psum_pool(name="psum", bufs=8))

        identity = keep.tile([P, P], F32)
        make_identity(nc, identity[:])
        by_frame = keep.tile([P, P], F32)

        as_it_lies = keep.tile([P, LOADS, STRIP], BF16)
        all_strips = video.rearrange("b f c h w -> (b f c h w)").rearrange("(s x) -> s x", x=STRIP)
        for row in range(2):
            cols = slice(row * GRID_ROW, (row + 1) * GRID_ROW)
            nc.sync.dma_start(out=as_it_lies[:, 0, cols], in_=all_strips[0:P, cols])
        for g in range(1, LOADS - 1):
            nc.sync.dma_start(out=as_it_lies[:, g, :], in_=all_strips[g * STRIPS : g * STRIPS + P, :])
        nc.sync.dma_start(out=as_it_lies[0:STRIPS, LOADS - 1, :], in_=strips[:, LOADS - 1, :])
        nc.sync.dma_start(out=as_it_lies[STRIPS:P, LOADS - 1, :], in_=all_strips[0 : P - STRIPS, :])
        raw_of_window = []
        for c in range(WINDOWS):
            raw = grad_in.tile([P, PACK, EMBED], BF16, name="raw")
            nc.sync.dma_start(
                out=raw[:].rearrange("p u e -> p (u e)"),
                in_=grad_rows[c * WINDOW : (c + 1) * WINDOW, :].rearrange("(p u) e -> p (u e)", u=PACK),
            )
            raw_of_window.append(raw)

        sorted_tiles = []
        for n in range(3):
            sorted_strips = keep.tile([P, STRIP_TOKENS, FRAME_FEATURES], BF16, name="sorted%d" % n)
            sorted_tiles.append(sorted_strips)

        by_feature = keep.tile([P, FRAMES, TOKENS], F32)
        tub_codes = keep.tile([P, WINDOWS, FEATURES], U32, align_bytes=64)
        tub_scales = keep.tile([P, WINDOWS, FEATURES], U8, align_bytes=64)

        def sort(g):
            sorted_strips = sorted_tiles[g % len(sorted_tiles)]
            for row in range(2):
                nc.vector.tensor_copy(
                    out=sorted_strips[:, row * GRID : (row + 1) * GRID, :].rearrange(
                        "p j (y x) -> p j y x", x=PATCH
                    ),
                    in_=as_it_lies[:, g, row * GRID_ROW : (row + 1) * GRID_ROW].rearrange(
                        "p (y j x) -> p j y x", j=GRID, x=PATCH
                    ),
                )

        def first_turn(g):
            words = sorted_tiles[g % len(sorted_tiles)][:].bitcast(F32)
            landing = by_feature[:, :, g * LOAD_TOKENS : (g + 1) * LOAD_TOKENS].rearrange(
                "p s (r q u) -> p q s r u", q=STRIP_TOKENS // PACK, u=PACK
            )
            for q in range(STRIP_TOKENS // PACK):
                bank = psum.tile([P, PACK, P], F32, tag="bank")
                for u in range(PACK):
                    nc.tensor.transpose(bank[:, u, :], words[:, q * PACK + u, :], by_frame[:])
                nc.scalar.copy(
                    out=landing[:, q],
                    in_=bank[:, :, 0:STRIPS].rearrange("p u (s r) -> p s r u", s=FRAMES),
                )

        def second_turn(c):
            grouped = stage.tile([P, FEATURES * PACK], BF16, name="grouped", align_bytes=64)
            for ts in range(FRAMES):
                window = by_feature[:, ts, c * WINDOW : (c + 1) * WINDOW].rearrange("p (m u) -> p u m", u=PACK)
                bank = psum.tile([P, PACK, P], F32, tag="bank")
                for u in range(PACK):
                    nc.tensor.transpose(bank[:, u, :], window[:, u, :], identity[:])
                frame_cols = slice(ts * FRAME_FEATURES * PACK, (ts + 1) * FRAME_FEATURES * PACK)
                copy = nc.vector.tensor_copy if ts == 1 else nc.scalar.copy
                copy(
                    out=grouped[:, frame_cols].rearrange("p (q u) -> p q u", u=PACK),
                    in_=bank[:].bitcast(BF16).rearrange("p u q -> p q u"),
                )
            return grouped

        def quantise_tubelets(c, grouped):
            nc.vector.quantize_mx(
                out=tub_codes[:, c, :].bitcast(E4M3_X4),
                scales=tub_scales[:, c, :],
                in_=grouped[:],
            )

        half = EMBED // 2
        halves = (slice(0, half), slice(half, EMBED))
        regrouped = []
        packed = []

        def regroup(c):
            raw = raw_of_window[c]
            side_by_side = grad_stage.tile([P, EMBED, PACK], BF16, name="side_by_side", align_bytes=64)
            vector_cols = {WINDOWS - 2: 432, WINDOWS - 1: 304}.get(c, 464)
            for cols, copy in (
                (slice(0, vector_cols), nc.vector.tensor_copy),
                (slice(vector_cols, half), nc.scalar.copy),
                (slice(half, EMBED), nc.scalar.copy),
            ):
                copy(
                    out=side_by_side[:, cols, :].rearrange("p (g r) u -> p g u r", r=4),
                    in_=raw[:, :, cols].rearrange("p u (g r) -> p g u r", r=4),
                )
            regrouped.append(side_by_side)

        def prepare(c):
            grad_codes = grad_packed.tile([P, EMBED], U32, name="grad_codes", align_bytes=64)
            grad_scales = grad_packed.tile([P, EMBED], U8, name="grad_scales", align_bytes=64)
            for h, cols in enumerate(halves):
                nc.vector.quantize_mx(
                    out=grad_codes[:, cols].bitcast(E5M2_X4),
                    scales=grad_scales[:, cols],
                    in_=regrouped[c][:, cols, :].rearrange("p e u -> p (e u)"),
                )
                if h == 0 and c + 1 < WINDOWS:
                    regroup(c + 1)
            packed.append((grad_codes, grad_scales))

        stack.enter_context(tc.manual_schedule())
        nc.vector.tensor_copy(out=by_frame[:, STRIPS:P], in_=identity[:, STRIPS:P])
        nc.vector.tensor_copy(
            out=by_frame[:, 0:STRIPS].rearrange("p (s a i) -> p s a i", s=FRAMES, i=STRIPS_PER_FRAME),
            in_=identity[:, 0:STRIPS].rearrange("p (a s i) -> p s a i", s=FRAMES, i=STRIPS_PER_FRAME),
        )
        turned = []
        quantised = 0
        sort(0)
        first_turn(0)
        sort(1)
        for g in range(LOADS):
            if g + 1 < LOADS:
                first_turn(g + 1)
            if g + 2 < LOADS:
                sort(g + 2)
            while len(turned) < WINDOWS and (len(turned) + 1) * WINDOW <= (g + 1) * LOAD_TOKENS:
                turned.append(second_turn(len(turned)))
                if len(turned) - quantised > 1:
                    quantise_tubelets(quantised, turned[quantised])
                    quantised += 1
            if g == LOADS - 3:
                regroup(0)
            if g == LOADS - 2:
                prepare(0)

        sums = [psum.tile([P, FEATURES], F32, name="sums%d" % m, tag="bank") for m in range(EMBED_TILES)]
        for c in range(WINDOWS):
            if c + 1 < WINDOWS:
                prepare(c + 1)
            if quantised < WINDOWS:
                quantise_tubelets(quantised, turned[quantised])
                quantised += 1
            grad_codes, grad_scales = packed[c]
            for m in range(EMBED_TILES):
                cols = slice(m * P, (m + 1) * P)
                nc.tensor.matmul_mx(
                    out=sums[m][:],
                    lhsT=grad_codes[:, cols].bitcast(E5M2_X4),
                    lhsT_scale=grad_scales[:, cols],
                    rhs=tub_codes[:, c, :].bitcast(E4M3_X4),
                    rhs_scale=tub_scales[:, c, :],
                    start=(c == 0),
                    stop=(c == WINDOWS - 1),
                )

        for m in range(EMBED_TILES):
            result = results.tile([P, FEATURES], F32)
            copy = nc.vector.tensor_copy if m % 2 == 0 else nc.scalar.copy
            copy(out=result[:], in_=sums[m][:])
            nc.sync.dma_start(out=out[m * P : (m + 1) * P, :], in_=result[:])
